import numpy as np
import ml_dtypes


def mxq(x, axis, fmt="e4m3"):
    dtype, down = {"e4m3": (ml_dtypes.float8_e4m3fn, 7), "e5m2": (ml_dtypes.float8_e5m2, 14)}[fmt]
    v = np.moveaxis(np.asarray(x, np.float32).astype(ml_dtypes.bfloat16).astype(np.float64), axis, -1)
    blocks = v.reshape(v.shape[:-1] + (-1, 32))
    amax = np.abs(blocks).max(-1, keepdims=True)
    byte = np.maximum(np.where(amax > 0, np.frexp(amax)[1] - 1 + 127, 0) - down, 1)
    scale = np.exp2(byte - 127.0)
    codes = (blocks / scale).astype(np.float32).astype(dtype).astype(np.float64)
    return np.moveaxis((codes * scale).reshape(v.shape), -1, axis)


WIDE = False


def mx_kscale(k):
    if not WIDE:
        return np.ones(k)
    levels = np.array([10, -10, 5, -5, 0])
    a = np.random.permutation(np.resize(levels, k // 512 * 4)).reshape(k // 512, 4)
    idx = np.arange(k)
    return np.exp2(a[idx // 512, idx % 128 // 32])


BF16 = ml_dtypes.bfloat16


def bf(x):
    return np.asarray(x, np.float32).astype(BF16)


def f64(x):
    return np.asarray(x).astype(np.float64)


B, SQ, SK, D, DK, L = 2, 8192, 256, 512, 64, 10000
P = max(SQ, SK)


def setup_inputs():
    s, t = mx_kscale(D), mx_kscale(D)
    return {"pe": bf(np.random.standard_normal((P, D)) * s),
            "Uq": bf(np.random.standard_normal((D, D)) * 0.6 / np.sqrt(D) / s[:, None] * t),
            "Uk": bf(np.random.standard_normal((D, D)) * 0.6 / np.sqrt(D) / s[:, None] / t)}


def reference(pe, Uq, Uk):
    peq = mxq(f64(pe), 1, "e4m3")
    q_pe = peq[:SQ] @ mxq(f64(Uq), 0, "e4m3")
    k_pe = peq[:SK] @ mxq(f64(Uk), 0, "e4m3")
    return mxq(q_pe, 1, "e4m3") @ mxq(k_pe, 1, "e4m3").T

@@ -1,0 +1,192 @@
+from contextlib import ExitStack
+
+import concourse.masks as masks
+import concourse.mybir as mybir
+
+BF16 = mybir.dt.bfloat16
+F32 = mybir.dt.float32
+U32 = mybir.dt.uint32
+U8 = mybir.dt.uint8
+FP8X4 = mybir.dt.float8_e4m3fn_x4
+
+P = 128
+PACK = 4
+SQ, SK, D = 8192, 256, 512
+BANK = 512
+WORDS = D // 2
+
+CHUNK_ROWS = 4
+KEY_ROWS = SK // P
+CHUNK = CHUNK_ROWS * P
+N_CHUNKS = SQ // CHUNK
+
+KEYS = 0
+N_JOBS = N_CHUNKS + 1
+
+FLOPS = 2 * D * (SQ * D + SK * D + SQ * SK)
+
+
+def tile_multiheadattention_tupe_pa_t_kernel(tc, pe, Uq, Uk, out):
+    nc = tc.nc
+    with ExitStack() as ctx:
+        keep = ctx.enter_context(tc.tile_pool(name="keep", bufs=1))
+        rows_in = ctx.enter_context(tc.tile_pool(name="rows_in", bufs=N_CHUNKS))
+        work = ctx.enter_context(tc.tile_pool(name="work", bufs=3))
+        rows_out = ctx.enter_context(tc.tile_pool(name="rows_out", bufs=4))
+        psum_x = ctx.enter_context(tc.psum_pool(name="psum_x", bufs=2))
+        psum_y = ctx.enter_context(tc.psum_pool(name="psum_y", bufs=4))
+        psum_s = ctx.enter_context(tc.psum_pool(name="psum_s", bufs=2))
+        ctx.enter_context(tc.manual_schedule())
+
+        def job_rows(job):
+            return KEY_ROWS if job == KEYS else CHUNK_ROWS
+
+        def empty_bank(bank, out_ap, in_ap):
+            if bank == 0:
+                nc.vector.tensor_copy(out=out_ap, in_=in_ap)
+            else:
+                nc.scalar.copy(out=out_ap, in_=in_ap)
+
+        def quantise(grouped, pool, tag):
+            width = grouped.shape[1] // PACK
+            codes = pool.tile([P, width], U32, tag=tag + "_codes", align_bytes=64)
+            scales = pool.tile([P, width], U8, tag=tag + "_scales", align_bytes=64)
+            nc.vector.quantize_mx(out=codes[:].bitcast(FP8X4), scales=scales[:], in_=grouped[:])
+            return codes, scales
+
+        def load_weights(w, tag):
+            raw = keep.tile([P, PACK, D], BF16, tag=tag + "_raw")
+            nc.sync.dma_start(
+                out=raw[:].rearrange("q (u e) c -> q u (e c)", u=2),
+                in_=w.rearrange("(u q e) c -> q u (e c)", u=2, e=2),
+            )
+            return raw
+
+        pe_rows = {}
+        uk_raw = load_weights(Uk, "uk")
+        key_rows = keep.tile([P, KEY_ROWS * D], BF16, tag="key_rows")
+        nc.sync.dma_start(
+            out=key_rows[:].rearrange("p (r d) -> p r d", r=KEY_ROWS),
+            in_=pe[0:SK, :].rearrange("(r p) d -> p r d", p=P),
+        )
+        pe_rows[KEYS] = key_rows
+        uq_raw = load_weights(Uq, "uq")
+        for job in range(1, N_JOBS):
+            first = (job - 1) * CHUNK
+            chunk_rows = rows_in.tile([P, CHUNK_ROWS * D], BF16, tag="chunk_rows")
+            nc.sync.dma_start(
+                out=chunk_rows[:],
+                in_=pe[first : first + CHUNK, :].rearrange("(p r) d -> p (r d)", r=CHUNK_ROWS),
+            )
+            pe_rows[job] = chunk_rows
+
+        identity = keep.tile([P, P], F32, tag="identity")
+        masks.make_identity(nc, identity[:])
+
+        def regroup_weights(copy, raw, tag):
+            grouped = keep.tile([P, PACK * D], BF16, tag=tag + "_grouped", align_bytes=64)
+            copy(
+                out=grouped[:].rearrange("q (f m t) -> q m t f", f=PACK, t=PACK),
+                in_=raw[:].rearrange("q t (m f) -> q m t f", f=PACK),
+            )
+            return grouped
+
+        uk_grouped = regroup_weights(nc.vector.tensor_copy, uk_raw, "uk")
+        uq_grouped = regroup_weights(nc.scalar.copy, uq_raw, "uq")
+        weights = {}
+
+        x_grouped, x_mx, y_grouped, y_mx = {}, {}, {}, {}
+
+        def transpose_features(job):
+            words = pe_rows[job][:].bitcast(F32)
+            grouped = work.tile([P, job_rows(job) * P * PACK], BF16, tag="x_grouped", align_bytes=64)
+            grouped_words = grouped[:].bitcast(F32)
+            for bank in range(job_rows(job) // 2):
+                xt = psum_x.tile([P, 2, 2 * P], F32, tag="xt")
+                for r in range(2):
+                    for u in range(2):
+                        first = ((2 * bank + r) * 2 + u) * P
+                        nc.tensor.transpose(
+                            xt[:, u, r * P : (r + 1) * P], words[:, first : first + P], identity[:]
+                        )
+                empty_bank(
+                    bank,
+                    grouped_words[:, bank * BANK : (bank + 1) * BANK].rearrange(
+                        "q (w u) -> q w u", u=2
+                    ),
+                    xt[:].rearrange("q u w -> q w u"),
+                )
+            x_grouped[job] = grouped
+
+        def project(job):
+            w_codes, w_scales = weights[job == KEYS]
+            x_codes, x_scales = x_mx[job]
+            grouped = work.tile([P, job_rows(job) * P * PACK], BF16, tag="y_grouped", align_bytes=64)
+            for bank in range(job_rows(job)):
+                cols = slice(bank * P, (bank + 1) * P)
+                yt = psum_y.tile([P, PACK, P], F32, tag="yt")
+                for f in range(PACK):
+                    feats = slice(f * P, (f + 1) * P)
+                    nc.tensor.matmul_mx(
+                        out=yt[:, f, :],
+                        lhsT=w_codes[:, feats].bitcast(FP8X4),
+                        lhsT_scale=w_scales[:, feats],
+                        rhs=x_codes[:, cols].bitcast(FP8X4),
+                        rhs_scale=x_scales[:, cols],
+                        start=True,
+                        stop=True,
+                    )
+                empty_bank(
+                    bank,
+                    grouped[:, bank * BANK : (bank + 1) * BANK].rearrange(
+                        "m (w f) -> m w f", f=PACK
+                    ),
+                    yt[:].rearrange("m f w -> m w f"),
+                )
+            y_grouped[job] = grouped
+
+        def score(job):
+            q_codes, q_scales = y_mx[job]
+            k_codes, k_scales = y_mx[KEYS]
+            result = rows_out.tile([P, CHUNK_ROWS * SK], F32, tag="result")
+            for bank in range(CHUNK_ROWS // 2):
+                st = psum_s.tile([P, 2, SK], F32, tag="st")
+                for r in range(2):
+                    cols = slice((2 * bank + r) * P, (2 * bank + r + 1) * P)
+                    nc.tensor.matmul_mx(
+                        out=st[:, r, :],
+                        lhsT=q_codes[:, cols].bitcast(FP8X4),
+                        lhsT_scale=q_scales[:, cols],
+                        rhs=k_codes[:].bitcast(FP8X4),
+                        rhs_scale=k_scales[:],
+                        start=True,
+                        stop=True,
+                    )
+                empty_bank(
+                    bank,
+                    result[:, bank * BANK : (bank + 1) * BANK],
+                    st[:].rearrange("p r n -> p (r n)"),
+                )
+            first = (job - 1) * CHUNK
+            nc.sync.dma_start(
+                out=out[first : first + CHUNK, :].rearrange("(p r) n -> p (r n)", r=CHUNK_ROWS),
+                in_=result[:],
+            )
+
+        for step in range(N_JOBS + 3):
+            if step < N_JOBS:
+                transpose_features(step)
+            if KEYS < step - 3 < N_JOBS:
+                score(step - 3)
+            if 0 <= step - 2 < N_JOBS:
+                y_mx[step - 2] = quantise(
+                    y_grouped[step - 2], keep if step - 2 == KEYS else work, "k" if step - 2 == KEYS else "q"
+                )
+            if step - 1 == KEYS:
+                weights[True] = quantise(uk_grouped, keep, "uk")
+            if step - 1 == KEYS + 1:
+                weights[False] = quantise(uq_grouped, keep, "uq")
+            if 0 <= step - 1 < N_JOBS:
+                project(step - 1)
+            if step < N_JOBS:
+                x_mx[step] = quantise(x_grouped[step], work, "x")

@@ -13,7 +13,6 @@ P = 128
 PACK = 4
 SQ, SK, D = 8192, 256, 512
 BANK = 512
-WORDS = D // 2
 
 CHUNK_ROWS = 4
 KEY_ROWS = SK // P
@@ -22,6 +21,10 @@ N_CHUNKS = SQ // CHUNK
 
 KEYS = 0
 N_JOBS = N_CHUNKS + 1
+
+PROJECT_LAG = 1
+REQUANTISE_LAG = 2
+SCORE_LAG = 3
 
 FLOPS = 2 * D * (SQ * D + SK * D + SQ * SK)
 
@@ -32,7 +35,7 @@ def tile_multiheadattention_tupe_pa_t_kernel(tc, pe, Uq, Uk, out):
         keep = ctx.enter_context(tc.tile_pool(name="keep", bufs=1))
         rows_in = ctx.enter_context(tc.tile_pool(name="rows_in", bufs=N_CHUNKS))
         work = ctx.enter_context(tc.tile_pool(name="work", bufs=3))
-        rows_out = ctx.enter_context(tc.tile_pool(name="rows_out", bufs=4))
+        rows_out = ctx.enter_context(tc.tile_pool(name="rows_out", bufs=8))
         psum_x = ctx.enter_context(tc.psum_pool(name="psum_x", bufs=2))
         psum_y = ctx.enter_context(tc.psum_pool(name="psum_y", bufs=4))
         psum_s = ctx.enter_context(tc.psum_pool(name="psum_s", bufs=2))
@@ -41,8 +44,8 @@ def tile_multiheadattention_tupe_pa_t_kernel(tc, pe, Uq, Uk, out):
         def job_rows(job):
             return KEY_ROWS if job == KEYS else CHUNK_ROWS
 
-        def empty_bank(bank, out_ap, in_ap):
-            if bank == 0:
+        def empty_bank(job, bank, out_ap, in_ap):
+            if bank == 0 and job != KEYS:
                 nc.vector.tensor_copy(out=out_ap, in_=in_ap)
             else:
                 nc.scalar.copy(out=out_ap, in_=in_ap)
@@ -62,15 +65,15 @@ def tile_multiheadattention_tupe_pa_t_kernel(tc, pe, Uq, Uk, out):
             )
             return raw
 
-        pe_rows = {}
+        uq_raw = load_weights(Uq, "uq")
         uk_raw = load_weights(Uk, "uk")
+        pe_rows = {}
         key_rows = keep.tile([P, KEY_ROWS * D], BF16, tag="key_rows")
         nc.sync.dma_start(
             out=key_rows[:].rearrange("p (r d) -> p r d", r=KEY_ROWS),
             in_=pe[0:SK, :].rearrange("(r p) d -> p r d", p=P),
         )
         pe_rows[KEYS] = key_rows
-        uq_raw = load_weights(Uq, "uq")
         for job in range(1, N_JOBS):
             first = (job - 1) * CHUNK
             chunk_rows = rows_in.tile([P, CHUNK_ROWS * D], BF16, tag="chunk_rows")
@@ -83,17 +86,19 @@ def tile_multiheadattention_tupe_pa_t_kernel(tc, pe, Uq, Uk, out):
         identity = keep.tile([P, P], F32, tag="identity")
         masks.make_identity(nc, identity[:])
 
-        def regroup_weights(copy, raw, tag):
+        def regroup_weights(raw, tag):
             grouped = keep.tile([P, PACK * D], BF16, tag=tag + "_grouped", align_bytes=64)
-            copy(
-                out=grouped[:].rearrange("q (f m t) -> q m t f", f=PACK, t=PACK),
-                in_=raw[:].rearrange("q t (m f) -> q m t f", f=PACK),
-            )
+            dst = grouped[:].rearrange("q (f m t) -> q m t f", f=PACK, t=PACK)
+            src = raw[:].rearrange("q t (m f) -> q m t f", f=PACK)
+            half = P // 2
+            nc.vector.tensor_copy(out=dst[:, :half], in_=src[:, :half])
+            nc.scalar.copy(out=dst[:, half:], in_=src[:, half:])
             return grouped
 
-        uk_grouped = regroup_weights(nc.vector.tensor_copy, uk_raw, "uk")
-        uq_grouped = regroup_weights(nc.scalar.copy, uq_raw, "uq")
-        weights = {}
+        uq_grouped = regroup_weights(uq_raw, "uq")
+        uk_grouped = regroup_weights(uk_raw, "uk")
+        uq_mx = quantise(uq_grouped, keep, "uq")
+        uk_mx = quantise(uk_grouped, keep, "uk")
 
         x_grouped, x_mx, y_grouped, y_mx = {}, {}, {}, {}
 
@@ -110,6 +115,7 @@ def tile_multiheadattention_tupe_pa_t_kernel(tc, pe, Uq, Uk, out):
                             xt[:, u, r * P : (r + 1) * P], words[:, first : first + P], identity[:]
                         )
                 empty_bank(
+                    job,
                     bank,
                     grouped_words[:, bank * BANK : (bank + 1) * BANK].rearrange(
                         "q (w u) -> q w u", u=2
@@ -119,7 +125,7 @@ def tile_multiheadattention_tupe_pa_t_kernel(tc, pe, Uq, Uk, out):
             x_grouped[job] = grouped
 
         def project(job):
-            w_codes, w_scales = weights[job == KEYS]
+            w_codes, w_scales = uk_mx if job == KEYS else uq_mx
             x_codes, x_scales = x_mx[job]
             grouped = work.tile([P, job_rows(job) * P * PACK], BF16, tag="y_grouped", align_bytes=64)
             for bank in range(job_rows(job)):
@@ -137,6 +143,7 @@ def tile_multiheadattention_tupe_pa_t_kernel(tc, pe, Uq, Uk, out):
                         stop=True,
                     )
                 empty_bank(
+                    job,
                     bank,
                     grouped[:, bank * BANK : (bank + 1) * BANK].rearrange(
                         "m (w f) -> m w f", f=PACK
@@ -148,7 +155,10 @@ def tile_multiheadattention_tupe_pa_t_kernel(tc, pe, Uq, Uk, out):
         def score(job):
             q_codes, q_scales = y_mx[job]
             k_codes, k_scales = y_mx[KEYS]
-            result = rows_out.tile([P, CHUNK_ROWS * SK], F32, tag="result")
+            first = (job - 1) * CHUNK
+            out_rows = out[first : first + CHUNK, :].rearrange(
+                "(p b r) n -> p b (r n)", b=CHUNK_ROWS // 2, r=2
+            )
             for bank in range(CHUNK_ROWS // 2):
                 st = psum_s.tile([P, 2, SK], F32, tag="st")
                 for r in range(2):
@@ -162,31 +172,20 @@ def tile_multiheadattention_tupe_pa_t_kernel(tc, pe, Uq, Uk, out):
                         start=True,
                         stop=True,
                     )
-                empty_bank(
-                    bank,
-                    result[:, bank * BANK : (bank + 1) * BANK],
-                    st[:].rearrange("p r n -> p (r n)"),
-                )
-            first = (job - 1) * CHUNK
-            nc.sync.dma_start(
-                out=out[first : first + CHUNK, :].rearrange("(p r) n -> p (r n)", r=CHUNK_ROWS),
-                in_=result[:],
-            )
+                result = rows_out.tile([P, BANK], F32, tag="result")
+                empty_bank(job, bank, result[:], st[:].rearrange("p r n -> p (r n)"))
+                nc.sync.dma_start(out=out_rows[:, bank, :], in_=result[:])
 
-        for step in range(N_JOBS + 3):
+        for step in range(N_JOBS + SCORE_LAG):
             if step < N_JOBS:
                 transpose_features(step)
-            if KEYS < step - 3 < N_JOBS:
-                score(step - 3)
-            if 0 <= step - 2 < N_JOBS:
-                y_mx[step - 2] = quantise(
-                    y_grouped[step - 2], keep if step - 2 == KEYS else work, "k" if step - 2 == KEYS else "q"
-                )
-            if step - 1 == KEYS:
-                weights[True] = quantise(uk_grouped, keep, "uk")
-            if step - 1 == KEYS + 1:
-                weights[False] = quantise(uq_grouped, keep, "uq")
-            if 0 <= step - 1 < N_JOBS:
-                project(step - 1)
+            if KEYS < step - SCORE_LAG < N_JOBS:
+                score(step - SCORE_LAG)
+            if step - REQUANTISE_LAG == KEYS:
+                y_mx[KEYS] = quantise(y_grouped[KEYS], keep, "k")
+            if KEYS < step - REQUANTISE_LAG < N_JOBS:
+                y_mx[step - REQUANTISE_LAG] = quantise(y_grouped[step - REQUANTISE_LAG], work, "q")
+            if 0 <= step - PROJECT_LAG < N_JOBS:
+                project(step - PROJECT_LAG)
             if step < N_JOBS:
                 x_mx[step] = quantise(x_grouped[step], work, "x")

@@ -35,7 +35,7 @@ def tile_multiheadattention_tupe_pa_t_kernel(tc, pe, Uq, Uk, out):
         keep = ctx.enter_context(tc.tile_pool(name="keep", bufs=1))
         rows_in = ctx.enter_context(tc.tile_pool(name="rows_in", bufs=N_CHUNKS))
         work = ctx.enter_context(tc.tile_pool(name="work", bufs=3))
-        rows_out = ctx.enter_context(tc.tile_pool(name="rows_out", bufs=8))
+        rows_out = ctx.enter_context(tc.tile_pool(name="rows_out", bufs=2 * N_CHUNKS))
         psum_x = ctx.enter_context(tc.psum_pool(name="psum_x", bufs=2))
         psum_y = ctx.enter_context(tc.psum_pool(name="psum_y", bufs=4))
         psum_s = ctx.enter_context(tc.psum_pool(name="psum_s", bufs=2))
@@ -44,8 +44,8 @@ def tile_multiheadattention_tupe_pa_t_kernel(tc, pe, Uq, Uk, out):
         def job_rows(job):
             return KEY_ROWS if job == KEYS else CHUNK_ROWS
 
-        def empty_bank(job, bank, out_ap, in_ap):
-            if bank == 0 and job != KEYS:
+        def empty_bank(by_vector, out_ap, in_ap):
+            if by_vector:
                 nc.vector.tensor_copy(out=out_ap, in_=in_ap)
             else:
                 nc.scalar.copy(out=out_ap, in_=in_ap)
@@ -115,8 +115,7 @@ def tile_multiheadattention_tupe_pa_t_kernel(tc, pe, Uq, Uk, out):
                             xt[:, u, r * P : (r + 1) * P], words[:, first : first + P], identity[:]
                         )
                 empty_bank(
-                    job,
-                    bank,
+                    job != KEYS,
                     grouped_words[:, bank * BANK : (bank + 1) * BANK].rearrange(
                         "q (w u) -> q w u", u=2
                     ),
@@ -143,8 +142,7 @@ def tile_multiheadattention_tupe_pa_t_kernel(tc, pe, Uq, Uk, out):
                         stop=True,
                     )
                 empty_bank(
-                    job,
-                    bank,
+                    False,
                     grouped[:, bank * BANK : (bank + 1) * BANK].rearrange(
                         "m (w f) -> m w f", f=PACK
                     ),
@@ -173,7 +171,7 @@ def tile_multiheadattention_tupe_pa_t_kernel(tc, pe, Uq, Uk, out):
                         stop=True,
                     )
                 result = rows_out.tile([P, BANK], F32, tag="result")
-                empty_bank(job, bank, result[:], st[:].rearrange("p r n -> p (r n)"))
+                empty_bank(bank == 0, result[:], st[:].rearrange("p r n -> p (r n)"))
                 nc.sync.dma_start(out=out_rows[:, bank, :], in_=result[:])
 
         for step in range(N_JOBS + SCORE_LAG):

from contextlib import ExitStack

import concourse.masks as masks
import concourse.mybir as mybir

BF16 = mybir.dt.bfloat16
F32 = mybir.dt.float32
U32 = mybir.dt.uint32
U8 = mybir.dt.uint8
FP8X4 = mybir.dt.float8_e4m3fn_x4

P = 128
PACK = 4
SQ, SK, D = 8192, 256, 512
BANK = 512

CHUNK_ROWS = 4
KEY_ROWS = SK // P
CHUNK = CHUNK_ROWS * P
N_CHUNKS = SQ // CHUNK

KEYS = 0
N_JOBS = N_CHUNKS + 1

PROJECT_LAG = 1
REQUANTISE_LAG = 2
SCORE_LAG = 3

FLOPS = 2 * D * (SQ * D + SK * D + SQ * SK)


def tile_multiheadattention_tupe_pa_t_kernel(tc, pe, Uq, Uk, out):
    nc = tc.nc
    with ExitStack() as ctx:
        keep = ctx.enter_context(tc.tile_pool(name="keep", bufs=1))
        rows_in = ctx.enter_context(tc.tile_pool(name="rows_in", bufs=N_CHUNKS))
        work = ctx.enter_context(tc.tile_pool(name="work", bufs=3))
        rows_out = ctx.enter_context(tc.tile_pool(name="rows_out", bufs=2 * N_CHUNKS))
        psum_x = ctx.enter_context(tc.psum_pool(name="psum_x", bufs=2))
        psum_y = ctx.enter_context(tc.psum_pool(name="psum_y", bufs=4))
        psum_s = ctx.enter_context(tc.psum_pool(name="psum_s", bufs=2))
        ctx.enter_context(tc.manual_schedule())

        def job_rows(job):
            return KEY_ROWS if job == KEYS else CHUNK_ROWS

        def empty_bank(by_vector, out_ap, in_ap):
            if by_vector:
                nc.vector.tensor_copy(out=out_ap, in_=in_ap)
            else:
                nc.scalar.copy(out=out_ap, in_=in_ap)

        def quantise(grouped, pool, tag):
            width = grouped.shape[1] // PACK
            codes = pool.tile([P, width], U32, tag=tag + "_codes", align_bytes=64)
            scales = pool.tile([P, width], U8, tag=tag + "_scales", align_bytes=64)
            nc.vector.quantize_mx(out=codes[:].bitcast(FP8X4), scales=scales[:], in_=grouped[:])
            return codes, scales

        def load_weights(w, tag):
            raw = keep.tile([P, PACK, D], BF16, tag=tag + "_raw")
            nc.sync.dma_start(
                out=raw[:].rearrange("q (u e) c -> q u (e c)", u=2),
                in_=w.rearrange("(u q e) c -> q u (e c)", u=2, e=2),
            )
            return raw

        uq_raw = load_weights(Uq, "uq")
        uk_raw = load_weights(Uk, "uk")
        pe_rows = {}
        key_rows = keep.tile([P, KEY_ROWS * D], BF16, tag="key_rows")
        nc.sync.dma_start(
            out=key_rows[:].rearrange("p (r d) -> p r d", r=KEY_ROWS),
            in_=pe[0:SK, :].rearrange("(r p) d -> p r d", p=P),
        )
        pe_rows[KEYS] = key_rows
        for job in range(1, N_JOBS):
            first = (job - 1) * CHUNK
            chunk_rows = rows_in.tile([P, CHUNK_ROWS * D], BF16, tag="chunk_rows")
            nc.sync.dma_start(
                out=chunk_rows[:],
                in_=pe[first : first + CHUNK, :].rearrange("(p r) d -> p (r d)", r=CHUNK_ROWS),
            )
            pe_rows[job] = chunk_rows

        identity = keep.tile([P, P], F32, tag="identity")
        masks.make_identity(nc, identity[:])

        def regroup_weights(raw, tag):
            grouped = keep.tile([P, PACK * D], BF16, tag=tag + "_grouped", align_bytes=64)
            dst = grouped[:].rearrange("q (f m t) -> q m t f", f=PACK, t=PACK)
            src = raw[:].rearrange("q t (m f) -> q m t f", f=PACK)
            half = P // 2
            nc.vector.tensor_copy(out=dst[:, :half], in_=src[:, :half])
            nc.scalar.copy(out=dst[:, half:], in_=src[:, half:])
            return grouped

        uq_grouped = regroup_weights(uq_raw, "uq")
        uk_grouped = regroup_weights(uk_raw, "uk")
        uq_mx = quantise(uq_grouped, keep, "uq")
        uk_mx = quantise(uk_grouped, keep, "uk")

        x_grouped, x_mx, y_grouped, y_mx = {}, {}, {}, {}

        def transpose_features(job):
            words = pe_rows[job][:].bitcast(F32)
            grouped = work.tile([P, job_rows(job) * P * PACK], BF16, tag="x_grouped", align_bytes=64)
            grouped_words = grouped[:].bitcast(F32)
            for bank in range(job_rows(job) // 2):
                xt = psum_x.tile([P, 2, 2 * P], F32, tag="xt")
                for r in range(2):
                    for u in range(2):
                        first = ((2 * bank + r) * 2 + u) * P
                        nc.tensor.transpose(
                            xt[:, u, r * P : (r + 1) * P], words[:, first : first + P], identity[:]
                        )
                empty_bank(
                    job != KEYS,
                    grouped_words[:, bank * BANK : (bank + 1) * BANK].rearrange(
                        "q (w u) -> q w u", u=2
                    ),
                    xt[:].rearrange("q u w -> q w u"),
                )
            x_grouped[job] = grouped

        def project(job):
            w_codes, w_scales = uk_mx if job == KEYS else uq_mx
            x_codes, x_scales = x_mx[job]
            grouped = work.tile([P, job_rows(job) * P * PACK], BF16, tag="y_grouped", align_bytes=64)
            for bank in range(job_rows(job)):
                cols = slice(bank * P, (bank + 1) * P)
                yt = psum_y.tile([P, PACK, P], F32, tag="yt")
                for f in range(PACK):
                    feats = slice(f * P, (f + 1) * P)
                    nc.tensor.matmul_mx(
                        out=yt[:, f, :],
                        lhsT=w_codes[:, feats].bitcast(FP8X4),
                        lhsT_scale=w_scales[:, feats],
                        rhs=x_codes[:, cols].bitcast(FP8X4),
                        rhs_scale=x_scales[:, cols],
                        start=True,
                        stop=True,
                    )
                empty_bank(
                    False,
                    grouped[:, bank * BANK : (bank + 1) * BANK].rearrange(
                        "m (w f) -> m w f", f=PACK
                    ),
                    yt[:].rearrange("m f w -> m w f"),
                )
            y_grouped[job] = grouped

        def score(job):
            q_codes, q_scales = y_mx[job]
            k_codes, k_scales = y_mx[KEYS]
            first = (job - 1) * CHUNK
            out_rows = out[first : first + CHUNK, :].rearrange(
                "(p b r) n -> p b (r n)", b=CHUNK_ROWS // 2, r=2
            )
            for bank in range(CHUNK_ROWS // 2):
                st = psum_s.tile([P, 2, SK], F32, tag="st")
                for r in range(2):
                    cols = slice((2 * bank + r) * P, (2 * bank + r + 1) * P)
                    nc.tensor.matmul_mx(
                        out=st[:, r, :],
                        lhsT=q_codes[:, cols].bitcast(FP8X4),
                        lhsT_scale=q_scales[:, cols],
                        rhs=k_codes[:].bitcast(FP8X4),
                        rhs_scale=k_scales[:],
                        start=True,
                        stop=True,
                    )
                result = rows_out.tile([P, BANK], F32, tag="result")
                empty_bank(bank == 0, result[:], st[:].rearrange("p r n -> p (r n)"))
                nc.sync.dma_start(out=out_rows[:, bank, :], in_=result[:])

        for step in range(N_JOBS + SCORE_LAG):
            if step < N_JOBS:
                transpose_features(step)
            if KEYS < step - SCORE_LAG < N_JOBS:
                score(step - SCORE_LAG)
            if step - REQUANTISE_LAG == KEYS:
                y_mx[KEYS] = quantise(y_grouped[KEYS], keep, "k")
            if KEYS < step - REQUANTISE_LAG < N_JOBS:
                y_mx[step - REQUANTISE_LAG] = quantise(y_grouped[step - REQUANTISE_LAG], work, "q")
            if 0 <= step - PROJECT_LAG < N_JOBS:
                project(step - PROJECT_LAG)
            if step < N_JOBS:
                x_mx[step] = quantise(x_grouped[step], work, "x")
